import numpy as np
import ml_dtypes


def mxq(x, axis, fmt="e4m3"):
    dtype, down = {"e4m3": (ml_dtypes.float8_e4m3fn, 7), "e5m2": (ml_dtypes.float8_e5m2, 14)}[fmt]
    v = np.moveaxis(np.asarray(x, np.float32).astype(ml_dtypes.bfloat16).astype(np.float64), axis, -1)
    blocks = v.reshape(v.shape[:-1] + (-1, 32))
    amax = np.abs(blocks).max(-1, keepdims=True)
    byte = np.maximum(np.where(amax > 0, np.frexp(amax)[1] - 1 + 127, 0) - down, 1)
    scale = np.exp2(byte - 127.0)
    codes = (blocks / scale).astype(np.float32).astype(dtype).astype(np.float64)
    return np.moveaxis((codes * scale).reshape(v.shape), -1, axis)


WIDE = False


def mx_kscale(k):
    if not WIDE:
        return np.ones(k)
    levels = np.array([10, -10, 5, -5, 0])
    a = np.random.permutation(np.resize(levels, k // 512 * 4)).reshape(k // 512, 4)
    idx = np.arange(k)
    return np.exp2(a[idx // 512, idx % 128 // 32])


BF16 = ml_dtypes.bfloat16


def bf(x):
    return np.asarray(x, np.float32).astype(BF16)


def f64(x):
    return np.asarray(x).astype(np.float64)


E2M1 = np.array([0.0, 0.5, 1.0, 1.5, 2.0, 3.0, 4.0, 6.0, -0.0, -0.5, -1.0, -1.5, -2.0, -3.0, -4.0, -6.0])


def pack_weight(w, fmt):
    k, n = w.shape
    w = f64(bf(w)).reshape(k // 32, 32, n)
    amax = np.abs(w).max(1)
    if fmt == "e4m3":
        byte = np.frexp(amax)[1] - 1 + 127 - 7
    else:
        mant, ex = np.frexp(amax / 6.0)
        byte = np.where(mant > 0.5, ex, ex - 1) + 127
    byte = np.clip(np.where(amax > 0, byte, 1), 1, 254)
    scaled = (w * np.exp2(127.0 - byte)[:, None, :]).reshape(k, n).astype(np.float32)
    by_word = np.ascontiguousarray(scaled.reshape(k // 512, 128, 4, n).transpose(0, 1, 3, 2))
    if fmt == "e4m3":
        words = by_word.astype(ml_dtypes.float8_e4m3fn).view(np.uint8)
    else:
        c = by_word.astype(ml_dtypes.float4_e2m1fn).view(np.uint8) & 0xF
        words = c[..., 0::2] | (c[..., 1::2] << 4)
    return np.ascontiguousarray(words), np.ascontiguousarray(byte.astype(np.uint8).reshape(k // 512, 16, n))


def unpack_weight(words, scales, fmt):
    g, p, n, _ = words.shape
    if fmt == "e4m3":
        vals = np.ascontiguousarray(words).view(ml_dtypes.float8_e4m3fn).astype(np.float64)
    else:
        nib = np.empty((g, p, n, 4), np.uint8)
        nib[..., 0::2] = words & 0xF
        nib[..., 1::2] = words >> 4
        vals = E2M1[nib]
    vals = vals * np.repeat(np.exp2(scales.astype(np.float64) - 127.0), 8, axis=1)[..., None]
    return vals.transpose(0, 1, 3, 2).reshape(g * 512, n)

def pack4(w):
    words, scales = pack_weight(w, "e2m1")
    return words.reshape(words.shape[0], 128, -1), scales


def unpack4(words, scales):
    return unpack_weight(words.reshape(words.shape[0], 128, -1, 2), scales, "e2m1")


B, C, H, W, M, O = 32, 512, 16, 16, 512, 128
N = B * H * W
L2_EPS = 1e-12
BN_EPS = 1e-5


def l2_normalize(x, axis):
    n = np.sqrt(np.sum(x * x, axis=axis, keepdims=True))
    return x / np.maximum(n, L2_EPS)


def setup_inputs():
    s = mx_kscale(C)
    cm = (np.random.standard_normal((N, C)) * 5.0 + np.random.standard_normal((1, C)) * 1.5) / np.sqrt(C)
    w = np.random.standard_normal((O, 2 * C)) * 0.1 / np.sqrt(2 * C)
    w[:, C:] = w[:, C:] / s
    words, scales = pack4(np.ascontiguousarray(w.T))
    return {"query": bf(np.random.standard_normal((B, C, H, W))), "concat_memory": bf(cm * s),
            "conv_w_words": words, "conv_w_scales": scales,
            "bn_gamma": bf(1.0 + 0.1 * np.random.standard_normal(O)), "bn_beta": bf(0.2 * np.random.standard_normal(O))}


def reference(query, concat_memory, conv_w_words, conv_w_scales, bn_gamma, bn_beta):
    q_flat = l2_normalize(f64(query), 1).transpose(0, 2, 3, 1).reshape(N, C)
    upd = np.concatenate([q_flat, f64(concat_memory)], axis=1)
    y = mxq(upd, 1, "e4m3") @ unpack4(conv_w_words, conv_w_scales)
    y = y.reshape(B, H, W, O).transpose(0, 3, 1, 2)
    mean = np.mean(y, axis=(0, 2, 3), keepdims=True)
    var = np.mean((y - mean) ** 2, axis=(0, 2, 3), keepdims=True)
    y = (y - mean) / np.sqrt(var + BN_EPS)
    y = y * f64(bn_gamma)[None, :, None, None] + f64(bn_beta)[None, :, None, None]
    return np.maximum(y, 0.0)

@@ -1,0 +1,210 @@
+from contextlib import ExitStack
+
+import concourse.mybir as mybir
+from concourse.masks import make_identity
+
+F32 = mybir.dt.float32
+BF16 = mybir.dt.bfloat16
+I32 = mybir.dt.int32
+U32 = mybir.dt.uint32
+U8 = mybir.dt.uint8
+FP8X4 = mybir.dt.float8_e4m3fn_x4
+FP4X4 = mybir.dt.float4_e2m1fn_x4
+ACT = mybir.ActivationFunctionType
+ALU = mybir.AluOpType
+
+P = 128
+PACK = 4
+BATCH, CHANNELS, PIXELS = 32, 512, 256
+OUT_CHANNELS = 128
+GROUPS = 2
+PAIRS = PIXELS // 2
+CHUNK_IMAGES = 2
+CHUNK_PIXELS = CHUNK_IMAGES * PIXELS
+CHUNKS = BATCH // CHUNK_IMAGES
+ROW_BLOCKS = CHUNK_PIXELS // P
+L2_EPS = 1e-12
+BN_EPS = 1e-5
+STATS = 6
+
+FLOPS = 2 * BATCH * PIXELS * GROUPS * CHANNELS * OUT_CHANNELS
+
+
+def tile_memory_sup_pb_t_kernel(
+    tc, query, concat_memory, conv_w_words, conv_w_scales, bn_gamma, bn_beta, out
+):
+    nc = tc.nc
+    with ExitStack() as stack:
+        keep = stack.enter_context(tc.tile_pool(name="keep", bufs=1))
+        loads = stack.enter_context(tc.tile_pool(name="loads", bufs=CHUNKS))
+        work = stack.enter_context(tc.tile_pool(name="work", bufs=3))
+        scrap = stack.enter_context(tc.tile_pool(name="scrap", bufs=4))
+        psum = stack.enter_context(tc.psum_pool(name="psum", bufs=2))
+        stack.enter_context(tc.manual_schedule())
+
+        ident = keep.tile([P, P], F32)
+        make_identity(nc, ident[:])
+        w_words = keep.tile([P, GROUPS, 2 * OUT_CHANNELS], U8, align_bytes=64)
+        w_scales = keep.tile([P, GROUPS, OUT_CHANNELS], U8, align_bytes=64)
+        nc.vector.memset(w_scales[:].bitcast(I32), 0)
+        gamma = keep.tile([P, 1], BF16)
+        beta = keep.tile([P, 1], BF16)
+        y_all = keep.tile([P, CHUNKS, CHUNK_PIXELS], F32)
+        stats = keep.tile([P, CHUNKS, STATS], F32)
+        minus_half = keep.tile([P, CHUNK_IMAGES, 2], F32)
+        nc.gpsimd.memset(minus_half[:], -0.5)
+
+        x_tiles = []
+        m_tiles = []
+        for c in range(CHUNKS):
+            x = loads.tile([P, CHUNK_IMAGES, PACK, PIXELS], BF16, name="x")
+            images = query[c * CHUNK_IMAGES : (c + 1) * CHUNK_IMAGES]
+            nc.sync.dma_start(
+                out=x[:].rearrange("p b t n -> p b (t n)"),
+                in_=images.rearrange("b (p t) h w -> p b (t h w)", t=PACK),
+            )
+            x_tiles.append(x)
+            m = loads.tile([P, ROW_BLOCKS, CHANNELS], BF16, name="m")
+            rows = concat_memory[c * CHUNK_PIXELS : (c + 1) * CHUNK_PIXELS, :]
+            nc.sync.dma_start(out=m[:], in_=rows.rearrange("(j p) k -> p j k", p=P))
+            m_tiles.append(m)
+            if c == 0:
+                nc.sync.dma_start(
+                    out=w_words[:].bitcast(I32),
+                    in_=conv_w_words.bitcast(I32).rearrange("g p n -> p g n"),
+                )
+                for quad in range(4):
+                    nc.sync.dma_start(
+                        out=w_scales[32 * quad : 32 * quad + 4].bitcast(I32),
+                        in_=conv_w_scales.bitcast(I32)[:, 4 * quad : 4 * quad + 4, :].rearrange(
+                            "g r n -> r g n"
+                        ),
+                    )
+                with nc.allow_non_contiguous_dma(reason="128 gains and shifts, one to a partition"):
+                    nc.scalar.dma_start(out=gamma[:], in_=bn_gamma.rearrange("(o one) -> o one", one=1))
+                    nc.scalar.dma_start(out=beta[:], in_=bn_beta.rearrange("(o one) -> o one", one=1))
+
+        inv_norms = {}
+        grouped = {}
+        operands = {}
+
+        def norms_and_memory(c):
+            x_words = x_tiles[c][:].bitcast(F32)
+            sumsq = work.tile([P, CHUNK_IMAGES, 2], F32, name="sumsq")
+            for b in range(CHUNK_IMAGES):
+                xt = psum.tile([P, PACK, P], F32, name="xt")
+                for t in range(PACK):
+                    nc.tensor.transpose(xt[:, t, :], x_words[:, b, t, :], ident[:])
+                by_pixel = xt[:].bitcast(BF16).rearrange("w t (p e) -> w t p e", e=2)
+                for e in range(2):
+                    squares = scrap.tile([P, PACK, P], BF16, name="squares")
+                    nc.scalar.activation(
+                        out=squares[:],
+                        in_=by_pixel[:, :, :, e],
+                        func=ACT.Square,
+                        accum_out=sumsq[:, b, e : e + 1],
+                    )
+            floored = work.tile([P, CHUNK_IMAGES, 2], F32, name="floored")
+            nc.gpsimd.tensor_scalar_max(out=floored[:], in0=sumsq[:], scalar1=L2_EPS * L2_EPS)
+            inv_norm = work.tile([P, CHUNK_IMAGES, 2], F32, name="inv_norm")
+            nc.gpsimd.tensor_tensor(out=inv_norm[:], in0=floored[:], in1=minus_half[:], op=ALU.pow)
+            inv_norms[c] = inv_norm
+
+            m_words = m_tiles[c][:].bitcast(F32)
+            gm = work.tile([P, ROW_BLOCKS, P, PACK], BF16, name="gm", align_bytes=64)
+            gm_words = gm[:].bitcast(F32)
+            for half in range(ROW_BLOCKS // 2):
+                mt = psum.tile([P, 2, 2, P], F32, name="mt")
+                for jj in range(2):
+                    for u in range(2):
+                        nc.tensor.transpose(
+                            mt[:, jj, u, :], m_words[:, 2 * half + jj, u : CHANNELS // 2 : 2], ident[:]
+                        )
+                nc.scalar.copy(
+                    out=gm_words[:, 2 * half : 2 * half + 2],
+                    in_=mt[:].rearrange("p j u r -> p j r u"),
+                )
+            grouped[c] = gm
+
+        def normalise_and_quantise(c):
+            inv_norm = inv_norms.pop(c)
+            spread = psum.tile([P, CHUNK_IMAGES, 2, PAIRS], F32, name="spread")
+            for b in range(CHUNK_IMAGES):
+                for e in range(2):
+                    nc.tensor.transpose(
+                        spread[:, b, e, :], inv_norm[:, b, e : e + 1].to_broadcast([P, P]), ident[:]
+                    )
+            gq = work.tile([P, CHUNK_IMAGES, PAIRS, 2, PACK], BF16, name="gq", align_bytes=64)
+            for b in range(CHUNK_IMAGES):
+                nc.vector.tensor_tensor(
+                    out=gq[:, b],
+                    in0=x_tiles[c][:, b].rearrange("p t (w e) -> p w e t", e=2),
+                    in1=spread[:, b].rearrange("p e w -> p w e").unsqueeze(3).to_broadcast([P, PAIRS, 2, PACK]),
+                    op=ALU.mult,
+                )
+            codes = work.tile([P, GROUPS, CHUNK_PIXELS], U32, name="codes", align_bytes=64)
+            scales = work.tile([P, GROUPS, CHUNK_PIXELS], U8, name="scales", align_bytes=64)
+            gm = grouped.pop(c)
+            nc.vector.quantize_mx(
+                out=codes[:, 1, :].bitcast(FP8X4),
+                scales=scales[:, 1, :],
+                in_=gm[:].rearrange("p j r t -> p (j r t)"),
+            )
+            nc.vector.quantize_mx(
+                out=codes[:, 0, :].bitcast(FP8X4),
+                scales=scales[:, 0, :],
+                in_=gq[:].rearrange("p b w e t -> p (b w e t)"),
+            )
+            operands[c] = (codes, scales)
+
+        def convolve(c):
+            codes, scales = operands.pop(c)
+            y = psum.tile([P, CHUNK_PIXELS], F32, name="y")
+            for g in range(GROUPS):
+                nc.tensor.matmul_mx(
+                    out=y[:],
+                    lhsT=w_words[:, g, :].bitcast(FP4X4),
+                    lhsT_scale=w_scales[:, g, :],
+                    rhs=codes[:, g, :].bitcast(FP8X4),
+                    rhs_scale=scales[:, g, :],
+                    start=(g == 0),
+                    stop=(g == GROUPS - 1),
+                )
+            nc.scalar.copy(out=y_all[:, c, :], in_=y[:])
+            nc.vector.bn_stats(out=stats[:, c, :], in_=y_all[:, c, :])
+
+        for step in range(CHUNKS + 2):
+            if step < CHUNKS:
+                norms_and_memory(step)
+            if 1 <= step <= CHUNKS:
+                normalise_and_quantise(step - 1)
+            if step >= 2:
+                convolve(step - 2)
+
+        mean_var = keep.tile([P, 2], F32)
+        nc.vector.bn_aggr(out=mean_var[:], in_=stats[:].rearrange("o c s -> o (c s)"))
+        var_eps = keep.tile([P, 1], F32)
+        nc.gpsimd.tensor_scalar_add(out=var_eps[:], in0=mean_var[:, 1:2], scalar1=BN_EPS)
+        rstd = keep.tile([P, 1], F32)
+        nc.gpsimd.tensor_tensor(out=rstd[:], in0=var_eps[:], in1=minus_half[:, 0, 0:1], op=ALU.pow)
+        neg_mean = keep.tile([P, 1], F32)
+        nc.vector.tensor_scalar_mul(out=neg_mean[:], in0=mean_var[:, 0:1], scalar1=-1.0)
+        scale = keep.tile([P, 1], F32)
+        nc.vector.tensor_tensor(out=scale[:], in0=gamma[:], in1=rstd[:], op=ALU.mult)
+        shift = keep.tile([P, 1], F32)
+        nc.vector.scalar_tensor_tensor(
+            out=shift[:], in0=neg_mean[:], scalar=scale[:, 0:1], in1=beta[:], op0=ALU.mult, op1=ALU.add
+        )
+        for c in range(CHUNKS):
+            y = y_all[:, c, :]
+            if c % 2 == 0:
+                nc.scalar.activation(out=y, in_=y, func=ACT.Relu, bias=shift[:, 0:1], scale=scale[:, 0:1])
+            else:
+                nc.vector.tensor_scalar(
+                    out=y, in0=y, scalar1=scale[:, 0:1], scalar2=shift[:, 0:1], op0=ALU.mult, op1=ALU.add
+                )
+                nc.vector.tensor_scalar_max(out=y, in0=y, scalar1=0.0)
+            nc.sync.dma_start(
+                out=out[c * CHUNK_IMAGES : (c + 1) * CHUNK_IMAGES].rearrange("b o h w -> o b (h w)"),
+                in_=y.rearrange("o (b n) -> o b n", b=CHUNK_IMAGES),
+            )

@@ -26,6 +26,8 @@ ROW_BLOCKS = CHUNK_PIXELS // P
 L2_EPS = 1e-12
 BN_EPS = 1e-5
 STATS = 6
+AHEAD = 6
+PSUM_BANKS = 8
 
 FLOPS = 2 * BATCH * PIXELS * GROUPS * CHANNELS * OUT_CHANNELS
 
@@ -36,10 +38,9 @@ def tile_memory_sup_pb_t_kernel(
     nc = tc.nc
     with ExitStack() as stack:
         keep = stack.enter_context(tc.tile_pool(name="keep", bufs=1))
-        loads = stack.enter_context(tc.tile_pool(name="loads", bufs=CHUNKS))
+        loads = stack.enter_context(tc.tile_pool(name="loads", bufs=AHEAD))
         work = stack.enter_context(tc.tile_pool(name="work", bufs=3))
         scrap = stack.enter_context(tc.tile_pool(name="scrap", bufs=4))
-        psum = stack.enter_context(tc.psum_pool(name="psum", bufs=2))
         stack.enter_context(tc.manual_schedule())
 
         ident = keep.tile([P, P], F32)
@@ -49,46 +50,49 @@ def tile_memory_sup_pb_t_kernel(
         nc.vector.memset(w_scales[:].bitcast(I32), 0)
         gamma = keep.tile([P, 1], BF16)
         beta = keep.tile([P, 1], BF16)
-        y_all = keep.tile([P, CHUNKS, CHUNK_PIXELS], F32)
+        result = keep.tile([P, CHUNKS, CHUNK_PIXELS], F32)
+        codes = keep.tile([P, CHUNKS, GROUPS, CHUNK_PIXELS], U32, align_bytes=64)
+        scales = keep.tile([P, CHUNKS, GROUPS, CHUNK_PIXELS], U8, align_bytes=64)
         stats = keep.tile([P, CHUNKS, STATS], F32)
         minus_half = keep.tile([P, CHUNK_IMAGES, 2], F32)
         nc.gpsimd.memset(minus_half[:], -0.5)
 
-        x_tiles = []
-        m_tiles = []
-        for c in range(CHUNKS):
+        x_tiles = {}
+        m_tiles = {}
+
+        def load(c):
             x = loads.tile([P, CHUNK_IMAGES, PACK, PIXELS], BF16, name="x")
             images = query[c * CHUNK_IMAGES : (c + 1) * CHUNK_IMAGES]
             nc.sync.dma_start(
                 out=x[:].rearrange("p b t n -> p b (t n)"),
                 in_=images.rearrange("b (p t) h w -> p b (t h w)", t=PACK),
             )
-            x_tiles.append(x)
+            x_tiles[c] = x
             m = loads.tile([P, ROW_BLOCKS, CHANNELS], BF16, name="m")
             rows = concat_memory[c * CHUNK_PIXELS : (c + 1) * CHUNK_PIXELS, :]
             nc.sync.dma_start(out=m[:], in_=rows.rearrange("(j p) k -> p j k", p=P))
-            m_tiles.append(m)
-            if c == 0:
-                nc.sync.dma_start(
-                    out=w_words[:].bitcast(I32),
-                    in_=conv_w_words.bitcast(I32).rearrange("g p n -> p g n"),
-                )
-                for quad in range(4):
-                    nc.sync.dma_start(
-                        out=w_scales[32 * quad : 32 * quad + 4].bitcast(I32),
-                        in_=conv_w_scales.bitcast(I32)[:, 4 * quad : 4 * quad + 4, :].rearrange(
-                            "g r n -> r g n"
-                        ),
-                    )
-                with nc.allow_non_contiguous_dma(reason="128 gains and shifts, one to a partition"):
-                    nc.scalar.dma_start(out=gamma[:], in_=bn_gamma.rearrange("(o one) -> o one", one=1))
-                    nc.scalar.dma_start(out=beta[:], in_=bn_beta.rearrange("(o one) -> o one", one=1))
+            m_tiles[c] = m
+
+        load(0)
+        nc.sync.dma_start(
+            out=w_words[:].bitcast(I32),
+            in_=conv_w_words.bitcast(I32).rearrange("g p n -> p g n"),
+        )
+        for quad in range(4):
+            nc.sync.dma_start(
+                out=w_scales[32 * quad : 32 * quad + 4].bitcast(I32),
+                in_=conv_w_scales.bitcast(I32)[:, 4 * quad : 4 * quad + 4, :].rearrange("g r n -> r g n"),
+            )
+        with nc.allow_non_contiguous_dma(reason="128 gains and shifts, one to a partition"):
+            nc.scalar.dma_start(out=gamma[:], in_=bn_gamma.rearrange("(o one) -> o one", one=1))
+            nc.scalar.dma_start(out=beta[:], in_=bn_beta.rearrange("(o one) -> o one", one=1))
+        for c in range(1, AHEAD):
+            load(c)
 
         inv_norms = {}
         grouped = {}
-        operands = {}
 
-        def norms_and_memory(c):
+        def norms_and_memory(c, psum):
             x_words = x_tiles[c][:].bitcast(F32)
             sumsq = work.tile([P, CHUNK_IMAGES, 2], F32, name="sumsq")
             for b in range(CHUNK_IMAGES):
@@ -126,7 +130,7 @@ def tile_memory_sup_pb_t_kernel(
                 )
             grouped[c] = gm
 
-        def normalise_and_quantise(c):
+        def normalise_and_quantise(c, psum):
             inv_norm = inv_norms.pop(c)
             spread = psum.tile([P, CHUNK_IMAGES, 2, PAIRS], F32, name="spread")
             for b in range(CHUNK_IMAGES):
@@ -142,44 +146,43 @@ def tile_memory_sup_pb_t_kernel(
                     in1=spread[:, b].rearrange("p e w -> p w e").unsqueeze(3).to_broadcast([P, PAIRS, 2, PACK]),
                     op=ALU.mult,
                 )
-            codes = work.tile([P, GROUPS, CHUNK_PIXELS], U32, name="codes", align_bytes=64)
-            scales = work.tile([P, GROUPS, CHUNK_PIXELS], U8, name="scales", align_bytes=64)
             gm = grouped.pop(c)
             nc.vector.quantize_mx(
-                out=codes[:, 1, :].bitcast(FP8X4),
-                scales=scales[:, 1, :],
+                out=codes[:, c, 1, :].bitcast(FP8X4),
+                scales=scales[:, c, 1, :],
                 in_=gm[:].rearrange("p j r t -> p (j r t)"),
             )
             nc.vector.quantize_mx(
-                out=codes[:, 0, :].bitcast(FP8X4),
-                scales=scales[:, 0, :],
+                out=codes[:, c, 0, :].bitcast(FP8X4),
+                scales=scales[:, c, 0, :],
                 in_=gq[:].rearrange("p b w e t -> p (b w e t)"),
             )
-            operands[c] = (codes, scales)
 
-        def convolve(c):
-            codes, scales = operands.pop(c)
-            y = psum.tile([P, CHUNK_PIXELS], F32, name="y")
+        def convolve(c, banks):
+            y = banks.tile([P, CHUNK_PIXELS], F32, name="y")
             for g in range(GROUPS):
                 nc.tensor.matmul_mx(
                     out=y[:],
                     lhsT=w_words[:, g, :].bitcast(FP4X4),
                     lhsT_scale=w_scales[:, g, :],
-                    rhs=codes[:, g, :].bitcast(FP8X4),
-                    rhs_scale=scales[:, g, :],
+                    rhs=codes[:, c, g, :].bitcast(FP8X4),
+                    rhs_scale=scales[:, c, g, :],
                     start=(g == 0),
                     stop=(g == GROUPS - 1),
                 )
-            nc.scalar.copy(out=y_all[:, c, :], in_=y[:])
-            nc.vector.bn_stats(out=stats[:, c, :], in_=y_all[:, c, :])
+            return y
 
-        for step in range(CHUNKS + 2):
-            if step < CHUNKS:
-                norms_and_memory(step)
-            if 1 <= step <= CHUNKS:
-                normalise_and_quantise(step - 1)
-            if step >= 2:
-                convolve(step - 2)
+        with tc.psum_pool(name="psum", bufs=2) as psum:
+            for step in range(CHUNKS + 2):
+                if step + AHEAD < CHUNKS:
+                    load(step + AHEAD)
+                if step < CHUNKS:
+                    norms_and_memory(step, psum)
+                if 1 <= step <= CHUNKS:
+                    normalise_and_quantise(step - 1, psum)
+                if step >= 2:
+                    y = convolve(step - 2, psum)
+                    nc.vector.bn_stats(out=stats[:, step - 2, :], in_=y[:])
 
         mean_var = keep.tile([P, 2], F32)
         nc.vector.bn_aggr(out=mean_var[:], in_=stats[:].rearrange("o c s -> o (c s)"))
@@ -195,16 +198,18 @@ def tile_memory_sup_pb_t_kernel(
         nc.vector.scalar_tensor_tensor(
             out=shift[:], in0=neg_mean[:], scalar=scale[:, 0:1], in1=beta[:], op0=ALU.mult, op1=ALU.add
         )
-        for c in range(CHUNKS):
-            y = y_all[:, c, :]
-            if c % 2 == 0:
-                nc.scalar.activation(out=y, in_=y, func=ACT.Relu, bias=shift[:, 0:1], scale=scale[:, 0:1])
-            else:
-                nc.vector.tensor_scalar(
-                    out=y, in0=y, scalar1=scale[:, 0:1], scalar2=shift[:, 0:1], op0=ALU.mult, op1=ALU.add
+        with tc.psum_pool(name="again", bufs=PSUM_BANKS, reuse_waits="tile") as again:
+            for c in range(CHUNKS):
+                y = convolve(c, again)
+                r = result[:, c, :]
+                if c % 2 == 0:
+                    nc.scalar.activation(out=r, in_=y[:], func=ACT.Relu, bias=shift[:, 0:1], scale=scale[:, 0:1])
+                else:
+                    nc.vector.tensor_scalar(
+                        out=r, in0=y[:], scalar1=scale[:, 0:1], scalar2=shift[:, 0:1], op0=ALU.mult, op1=ALU.add
+                    )
+                    nc.vector.tensor_scalar_max(out=r, in0=r, scalar1=0.0)
+                nc.sync.dma_start(
+                    out=out[c * CHUNK_IMAGES : (c + 1) * CHUNK_IMAGES].rearrange("b o h w -> o b (h w)"),
+                    in_=r.rearrange("o (b n) -> o b n", b=CHUNK_IMAGES),
                 )
-                nc.vector.tensor_scalar_max(out=y, in0=y, scalar1=0.0)
-            nc.sync.dma_start(
-                out=out[c * CHUNK_IMAGES : (c + 1) * CHUNK_IMAGES].rearrange("b o h w -> o b (h w)"),
-                in_=y.rearrange("o (b n) -> o b n", b=CHUNK_IMAGES),
-            )

@@ -28,6 +28,7 @@ BN_EPS = 1e-5
 STATS = 6
 AHEAD = 6
 PSUM_BANKS = 8
+LINE = 8
 
 FLOPS = 2 * BATCH * PIXELS * GROUPS * CHANNELS * OUT_CHANNELS
 
@@ -132,18 +133,19 @@ def tile_memory_sup_pb_t_kernel(
 
         def normalise_and_quantise(c, psum):
             inv_norm = inv_norms.pop(c)
-            spread = psum.tile([P, CHUNK_IMAGES, 2, PAIRS], F32, name="spread")
+            spread = psum.tile([P, CHUNK_IMAGES, PAIRS, 2], F32, name="spread")
             for b in range(CHUNK_IMAGES):
                 for e in range(2):
                     nc.tensor.transpose(
-                        spread[:, b, e, :], inv_norm[:, b, e : e + 1].to_broadcast([P, P]), ident[:]
+                        spread[:, b, :, e], inv_norm[:, b, e : e + 1].to_broadcast([P, P]), ident[:]
                     )
-            gq = work.tile([P, CHUNK_IMAGES, PAIRS, 2, PACK], BF16, name="gq", align_bytes=64)
+            gq = work.tile([P, CHUNK_IMAGES, PIXELS, PACK], BF16, name="gq", align_bytes=64)
             for b in range(CHUNK_IMAGES):
+                factor = spread[:, b].rearrange("p (l i) e -> p l (i e)", i=LINE // 2).unsqueeze(2)
                 nc.vector.tensor_tensor(
-                    out=gq[:, b],
-                    in0=x_tiles[c][:, b].rearrange("p t (w e) -> p w e t", e=2),
-                    in1=spread[:, b].rearrange("p e w -> p w e").unsqueeze(3).to_broadcast([P, PAIRS, 2, PACK]),
+                    out=gq[:, b].rearrange("p (l i) t -> p l t i", i=LINE),
+                    in0=x_tiles[c][:, b].rearrange("p t (l i) -> p l t i", i=LINE),
+                    in1=factor.to_broadcast([P, PIXELS // LINE, PACK, LINE]),
                     op=ALU.mult,
                 )
             gm = grouped.pop(c)
@@ -155,7 +157,7 @@ def tile_memory_sup_pb_t_kernel(
             nc.vector.quantize_mx(
                 out=codes[:, c, 0, :].bitcast(FP8X4),
                 scales=scales[:, c, 0, :],
-                in_=gq[:].rearrange("p b w e t -> p (b w e t)"),
+                in_=gq[:].rearrange("p b n t -> p (b n t)"),
             )
 
         def convolve(c, banks):

@@ -57,24 +57,38 @@ def tile_memory_sup_pb_t_kernel(
         stats = keep.tile([P, CHUNKS, STATS], F32)
         minus_half = keep.tile([P, CHUNK_IMAGES, 2], F32)
         nc.gpsimd.memset(minus_half[:], -0.5)
+        one = keep.tile([P, 1], F32)
+        nc.vector.memset(one[:], 1.0)
+        root_of_one = keep.tile([P, 1], F32)
+        nc.scalar.activation(out=root_of_one[:], in_=one[:], func=ACT.Sqrt)
 
         x_tiles = {}
         m_tiles = {}
 
-        def load(c):
-            x = loads.tile([P, CHUNK_IMAGES, PACK, PIXELS], BF16, name="x")
-            images = query[c * CHUNK_IMAGES : (c + 1) * CHUNK_IMAGES]
+        def load_pixels(c, image, images):
+            if c not in x_tiles:
+                x = loads.tile([P, CHUNK_IMAGES, PACK, PIXELS], BF16, name="x")
+                x_tiles[c] = x
+            first = c * CHUNK_IMAGES + image
             nc.sync.dma_start(
-                out=x[:].rearrange("p b t n -> p b (t n)"),
-                in_=images.rearrange("b (p t) h w -> p b (t h w)", t=PACK),
+                out=x_tiles[c][:, image : image + images].rearrange("p b t n -> p b (t n)"),
+                in_=query[first : first + images].rearrange("b (p t) h w -> p b (t h w)", t=PACK),
             )
-            x_tiles[c] = x
+
+        def load_memory(c):
             m = loads.tile([P, ROW_BLOCKS, CHANNELS], BF16, name="m")
             rows = concat_memory[c * CHUNK_PIXELS : (c + 1) * CHUNK_PIXELS, :]
             nc.sync.dma_start(out=m[:], in_=rows.rearrange("(j p) k -> p j k", p=P))
             m_tiles[c] = m
 
-        load(0)
+        def load(c):
+            load_pixels(c, 0, CHUNK_IMAGES)
+            load_memory(c)
+
+        for b in range(CHUNK_IMAGES):
+            load_pixels(0, b, 1)
+        load_memory(0)
+        load(1)
         nc.sync.dma_start(
             out=w_words[:].bitcast(I32),
             in_=conv_w_words.bitcast(I32).rearrange("g p n -> p g n"),
@@ -87,37 +101,52 @@ def tile_memory_sup_pb_t_kernel(
         with nc.allow_non_contiguous_dma(reason="128 gains and shifts, one to a partition"):
             nc.scalar.dma_start(out=gamma[:], in_=bn_gamma.rearrange("(o one) -> o one", one=1))
             nc.scalar.dma_start(out=beta[:], in_=bn_beta.rearrange("(o one) -> o one", one=1))
-        for c in range(1, AHEAD):
+        for c in range(2, AHEAD):
             load(c)
 
+        sums = {}
         inv_norms = {}
         grouped = {}
 
-        def norms_and_memory(c, psum):
-            x_words = x_tiles[c][:].bitcast(F32)
-            sumsq = work.tile([P, CHUNK_IMAGES, 2], F32, name="sumsq")
-            for b in range(CHUNK_IMAGES):
-                xt = psum.tile([P, PACK, P], F32, name="xt")
-                for t in range(PACK):
-                    nc.tensor.transpose(xt[:, t, :], x_words[:, b, t, :], ident[:])
-                by_pixel = xt[:].bitcast(BF16).rearrange("w t (p e) -> w t p e", e=2)
-                for e in range(2):
-                    squares = scrap.tile([P, PACK, P], BF16, name="squares")
-                    nc.scalar.activation(
-                        out=squares[:],
-                        in_=by_pixel[:, :, :, e],
-                        func=ACT.Square,
-                        accum_out=sumsq[:, b, e : e + 1],
-                    )
-            floored = work.tile([P, CHUNK_IMAGES, 2], F32, name="floored")
-            nc.gpsimd.tensor_scalar_max(out=floored[:], in0=sumsq[:], scalar1=L2_EPS * L2_EPS)
-            inv_norm = work.tile([P, CHUNK_IMAGES, 2], F32, name="inv_norm")
-            nc.gpsimd.tensor_tensor(out=inv_norm[:], in0=floored[:], in1=minus_half[:], op=ALU.pow)
-            inv_norms[c] = inv_norm
+        def operands(c):
+            if c not in grouped:
+                g = work.tile([P, GROUPS, CHUNK_PIXELS * PACK], BF16, name="g", align_bytes=64)
+                grouped[c] = g
+            return grouped[c]
 
+        def square_sums(c, b, psum):
+            if c not in sums:
+                sumsq = work.tile([P, CHUNK_IMAGES, 2], F32, name="sumsq")
+                sums[c] = sumsq
+            x_words = x_tiles[c][:].bitcast(F32)
+            xt = psum.tile([P, PACK, P], F32, name="xt")
+            for t in range(PACK):
+                nc.tensor.transpose(xt[:, t, :], x_words[:, b, t, :], ident[:])
+            by_pixel = xt[:].bitcast(BF16).rearrange("w t (p e) -> w t p e", e=2)
+            for e in range(2):
+                squares = scrap.tile([P, PACK, P], BF16, name="squares")
+                nc.scalar.activation(
+                    out=squares[:],
+                    in_=by_pixel[:, :, :, e],
+                    func=ACT.Square,
+                    accum_out=sums[c][:, b, e : e + 1],
+                )
+
+        def invert(c, image, images):
+            if c not in inv_norms:
+                inv_norm = work.tile([P, CHUNK_IMAGES, 2], F32, name="inv_norm")
+                inv_norms[c] = inv_norm
+            part = slice(image, image + images)
+            floored = work.tile([P, images, 2], F32, name="floored")
+            nc.gpsimd.tensor_scalar_max(out=floored[:], in0=sums[c][:, part], scalar1=L2_EPS * L2_EPS)
+            nc.gpsimd.tensor_tensor(
+                out=inv_norms[c][:, part], in0=floored[:], in1=minus_half[:, part], op=ALU.pow
+            )
+
+        def group_memory(c, psum, copy):
             m_words = m_tiles[c][:].bitcast(F32)
-            gm = work.tile([P, ROW_BLOCKS, P, PACK], BF16, name="gm", align_bytes=64)
-            gm_words = gm[:].bitcast(F32)
+            rows = operands(c)[:, 1].rearrange("p (j r t) -> p j r t", j=ROW_BLOCKS, t=PACK)
+            gm_words = rows.bitcast(F32)
             for half in range(ROW_BLOCKS // 2):
                 mt = psum.tile([P, 2, 2, P], F32, name="mt")
                 for jj in range(2):
@@ -125,39 +154,32 @@ def tile_memory_sup_pb_t_kernel(
                         nc.tensor.transpose(
                             mt[:, jj, u, :], m_words[:, 2 * half + jj, u : CHANNELS // 2 : 2], ident[:]
                         )
-                nc.scalar.copy(
+                copy(
                     out=gm_words[:, 2 * half : 2 * half + 2],
                     in_=mt[:].rearrange("p j u r -> p j r u"),
                 )
-            grouped[c] = gm
 
-        def normalise_and_quantise(c, psum):
-            inv_norm = inv_norms.pop(c)
-            spread = psum.tile([P, CHUNK_IMAGES, PAIRS, 2], F32, name="spread")
-            for b in range(CHUNK_IMAGES):
-                for e in range(2):
-                    nc.tensor.transpose(
-                        spread[:, b, :, e], inv_norm[:, b, e : e + 1].to_broadcast([P, P]), ident[:]
-                    )
-            gq = work.tile([P, CHUNK_IMAGES, PIXELS, PACK], BF16, name="gq", align_bytes=64)
-            for b in range(CHUNK_IMAGES):
-                factor = spread[:, b].rearrange("p (l i) e -> p l (i e)", i=LINE // 2).unsqueeze(2)
-                nc.vector.tensor_tensor(
-                    out=gq[:, b].rearrange("p (l i) t -> p l t i", i=LINE),
-                    in0=x_tiles[c][:, b].rearrange("p t (l i) -> p l t i", i=LINE),
-                    in1=factor.to_broadcast([P, PIXELS // LINE, PACK, LINE]),
-                    op=ALU.mult,
+        def normalise(c, b, psum):
+            spread = psum.tile([P, PAIRS, 2], F32, name="spread")
+            for e in range(2):
+                nc.tensor.transpose(
+                    spread[:, :, e], inv_norms[c][:, b, e : e + 1].to_broadcast([P, P]), ident[:]
                 )
-            gm = grouped.pop(c)
-            nc.vector.quantize_mx(
-                out=codes[:, c, 1, :].bitcast(FP8X4),
-                scales=scales[:, c, 1, :],
-                in_=gm[:].rearrange("p j r t -> p (j r t)"),
+            gq = operands(c)[:, 0].rearrange("p (b n t) -> p b n t", b=CHUNK_IMAGES, t=PACK)
+            factor = spread[:].rearrange("p (l i) e -> p l (i e)", i=LINE // 2).unsqueeze(2)
+            nc.vector.tensor_tensor(
+                out=gq[:, b].rearrange("p (l i) t -> p l t i", i=LINE),
+                in0=x_tiles[c][:, b].rearrange("p t (l i) -> p l t i", i=LINE),
+                in1=factor.to_broadcast([P, PIXELS // LINE, PACK, LINE]),
+                op=ALU.mult,
             )
+
+        def quantise(c):
+            g = grouped.pop(c)
             nc.vector.quantize_mx(
-                out=codes[:, c, 0, :].bitcast(FP8X4),
-                scales=scales[:, c, 0, :],
-                in_=gq[:].rearrange("p b n t -> p (b n t)"),
+                out=codes[:, c].rearrange("p g n -> p (g n)").bitcast(FP8X4),
+                scales=scales[:, c].rearrange("p g n -> p (g n)"),
+                in_=g[:].rearrange("p g n -> p (g n)"),
             )
 
         def convolve(c, banks):
@@ -175,23 +197,43 @@ def tile_memory_sup_pb_t_kernel(
             return y
 
         with tc.psum_pool(name="psum", bufs=2) as psum:
-            for step in range(CHUNKS + 2):
+            for b in range(CHUNK_IMAGES):
+                square_sums(0, b, psum)
+                invert(0, b, 1)
+            group_memory(0, psum, nc.vector.tensor_copy)
+            square_sums(1, 0, psum)
+            normalise(0, 0, psum)
+            square_sums(1, 1, psum)
+            invert(1, 0, CHUNK_IMAGES)
+            normalise(0, 1, psum)
+            group_memory(1, psum, nc.vector.tensor_copy)
+            quantise(0)
+            for c in range(AHEAD, AHEAD + 2):
+                load(c)
+            for step in range(2, CHUNKS + 2):
                 if step + AHEAD < CHUNKS:
                     load(step + AHEAD)
                 if step < CHUNKS:
-                    norms_and_memory(step, psum)
-                if 1 <= step <= CHUNKS:
-                    normalise_and_quantise(step - 1, psum)
-                if step >= 2:
-                    y = convolve(step - 2, psum)
-                    nc.vector.bn_stats(out=stats[:, step - 2, :], in_=y[:])
+                    for b in range(CHUNK_IMAGES):
+                        square_sums(step, b, psum)
+                    invert(step, 0, CHUNK_IMAGES)
+                    group_memory(step, psum, nc.scalar.copy)
+                if step <= CHUNKS:
+                    for b in range(CHUNK_IMAGES):
+                        normalise(step - 1, b, psum)
+                y = convolve(step - 2, psum)
+                nc.vector.bn_stats(out=stats[:, step - 2, :], in_=y[:])
+                if step <= CHUNKS:
+                    quantise(step - 1)
 
         mean_var = keep.tile([P, 2], F32)
         nc.vector.bn_aggr(out=mean_var[:], in_=stats[:].rearrange("o c s -> o (c s)"))
         var_eps = keep.tile([P, 1], F32)
-        nc.gpsimd.tensor_scalar_add(out=var_eps[:], in0=mean_var[:, 1:2], scalar1=BN_EPS)
+        nc.vector.tensor_scalar_add(out=var_eps[:], in0=mean_var[:, 1:2], scalar1=BN_EPS)
+        std = keep.tile([P, 1], F32)
+        nc.scalar.activation(out=std[:], in_=var_eps[:], func=ACT.Sqrt)
         rstd = keep.tile([P, 1], F32)
-        nc.gpsimd.tensor_tensor(out=rstd[:], in0=var_eps[:], in1=minus_half[:, 0, 0:1], op=ALU.pow)
+        nc.vector.reciprocal(out=rstd[:], in_=std[:])
         neg_mean = keep.tile([P, 1], F32)
         nc.vector.tensor_scalar_mul(out=neg_mean[:], in0=mean_var[:, 0:1], scalar1=-1.0)
         scale = keep.tile([P, 1], F32)

@@ -26,7 +26,7 @@ ROW_BLOCKS = CHUNK_PIXELS // P
 L2_EPS = 1e-12
 BN_EPS = 1e-5
 STATS = 6
-AHEAD = 6
+AHEAD = 7
 PSUM_BANKS = 8
 LINE = 8
 
@@ -208,23 +208,25 @@ def tile_memory_sup_pb_t_kernel(
             normalise(0, 1, psum)
             group_memory(1, psum, nc.vector.tensor_copy)
             quantise(0)
-            for c in range(AHEAD, AHEAD + 2):
-                load(c)
-            for step in range(2, CHUNKS + 2):
-                if step + AHEAD < CHUNKS:
-                    load(step + AHEAD)
+            load(AHEAD)
+            for step in range(2, CHUNKS + 3):
+                c = step - 2
+                if 1 <= c < CHUNKS:
+                    if c + AHEAD < CHUNKS:
+                        load(c + AHEAD)
+                    for b in range(CHUNK_IMAGES):
+                        normalise(c, b, psum)
                 if step < CHUNKS:
                     for b in range(CHUNK_IMAGES):
                         square_sums(step, b, psum)
                     invert(step, 0, CHUNK_IMAGES)
+                if c >= 1:
+                    y = convolve(c - 1, psum)
+                    nc.vector.bn_stats(out=stats[:, c - 1, :], in_=y[:])
+                if step < CHUNKS:
                     group_memory(step, psum, nc.scalar.copy)
-                if step <= CHUNKS:
-                    for b in range(CHUNK_IMAGES):
-                        normalise(step - 1, b, psum)
-                y = convolve(step - 2, psum)
-                nc.vector.bn_stats(out=stats[:, step - 2, :], in_=y[:])
-                if step <= CHUNKS:
-                    quantise(step - 1)
+                if 1 <= c < CHUNKS:
+                    quantise(c)
 
         mean_var = keep.tile([P, 2], F32)
         nc.vector.bn_aggr(out=mean_var[:], in_=stats[:].rearrange("o c s -> o (c s)"))

@@ -25,9 +25,11 @@ CHUNKS = BATCH // CHUNK_IMAGES
 ROW_BLOCKS = CHUNK_PIXELS // P
 L2_EPS = 1e-12
 BN_EPS = 1e-5
-STATS = 6
+RECORD = 3
+STATS = 2 * RECORD
+SCALAR_CHUNKS = range(CHUNKS - 4, CHUNKS - 1)
 AHEAD = 7
-PSUM_BANKS = 8
+BANK_TAGS = ("xt", "mt", "spread", "y")
 LINE = 8
 
 FLOPS = 2 * BATCH * PIXELS * GROUPS * CHANNELS * OUT_CHANNELS
@@ -54,9 +56,16 @@ def tile_memory_sup_pb_t_kernel(
         result = keep.tile([P, CHUNKS, CHUNK_PIXELS], F32)
         codes = keep.tile([P, CHUNKS, GROUPS, CHUNK_PIXELS], U32, align_bytes=64)
         scales = keep.tile([P, CHUNKS, GROUPS, CHUNK_PIXELS], U8, align_bytes=64)
-        stats = keep.tile([P, CHUNKS, STATS], F32)
+        vector_stats = (CHUNKS - len(SCALAR_CHUNKS)) * STATS
+        stats = keep.tile([P, vector_stats + len(SCALAR_CHUNKS) * RECORD], F32)
+        minus_shift = keep.tile([P, 1], F32)
+        shifted_sum = keep.tile([P, len(SCALAR_CHUNKS)], F32)
+        shifted_squares = keep.tile([P, len(SCALAR_CHUNKS)], F32)
         minus_half = keep.tile([P, CHUNK_IMAGES, 2], F32)
         nc.gpsimd.memset(minus_half[:], -0.5)
+        eps = keep.tile([P, 1], F32)
+        nc.vector.memset(eps[:], 0.0)
+        nc.vector.tensor_scalar_add(out=eps[:], in0=eps[:], scalar1=BN_EPS)
         one = keep.tile([P, 1], F32)
         nc.vector.memset(one[:], 1.0)
         root_of_one = keep.tile([P, 1], F32)
@@ -67,13 +76,13 @@ def tile_memory_sup_pb_t_kernel(
 
         def load_pixels(c, image, images):
             if c not in x_tiles:
-                x = loads.tile([P, CHUNK_IMAGES, PACK, PIXELS], BF16, name="x")
+                x = loads.tile([P, PACK, CHUNK_IMAGES, PIXELS], BF16, name="x")
                 x_tiles[c] = x
-            first = c * CHUNK_IMAGES + image
-            nc.sync.dma_start(
-                out=x_tiles[c][:, image : image + images].rearrange("p b t n -> p b (t n)"),
-                in_=query[first : first + images].rearrange("b (p t) h w -> p b (t h w)", t=PACK),
-            )
+            for b in range(image, image + images):
+                nc.sync.dma_start(
+                    out=x_tiles[c][:, :, b],
+                    in_=query[c * CHUNK_IMAGES + b].rearrange("(p t) h w -> p t (h w)", t=PACK),
+                )
 
         def load_memory(c):
             m = loads.tile([P, ROW_BLOCKS, CHANNELS], BF16, name="m")
@@ -121,7 +130,7 @@ def tile_memory_sup_pb_t_kernel(
             x_words = x_tiles[c][:].bitcast(F32)
             xt = psum.tile([P, PACK, P], F32, name="xt")
             for t in range(PACK):
-                nc.tensor.transpose(xt[:, t, :], x_words[:, b, t, :], ident[:])
+                nc.tensor.transpose(xt[:, t, :], x_words[:, t, b, :], ident[:])
             by_pixel = xt[:].bitcast(BF16).rearrange("w t (p e) -> w t p e", e=2)
             for e in range(2):
                 squares = scrap.tile([P, PACK, P], BF16, name="squares")
@@ -131,6 +140,7 @@ def tile_memory_sup_pb_t_kernel(
                     func=ACT.Square,
                     accum_out=sums[c][:, b, e : e + 1],
                 )
+            return by_pixel
 
         def invert(c, image, images):
             if c not in inv_norms:
@@ -159,18 +169,46 @@ def tile_memory_sup_pb_t_kernel(
                     in_=mt[:].rearrange("p j u r -> p j r u"),
                 )
 
-        def normalise(c, b, psum):
-            spread = psum.tile([P, PAIRS, 2], F32, name="spread")
+        def normalise_rows(c, b, by_pixel):
+            q_rows = work.tile([P, 2, CHANNELS], BF16, name="q_rows")
             for e in range(2):
-                nc.tensor.transpose(
-                    spread[:, :, e], inv_norms[c][:, b, e : e + 1].to_broadcast([P, P]), ident[:]
+                nc.scalar.activation(
+                    out=q_rows[:, e].rearrange("w (p t) -> w p t", t=PACK),
+                    in_=by_pixel[:, :, :, e].rearrange("w t p -> w p t"),
+                    func=ACT.Copy,
+                    scale=inv_norms[c][:, b, e : e + 1],
                 )
-            gq = operands(c)[:, 0].rearrange("p (b n t) -> p b n t", b=CHUNK_IMAGES, t=PACK)
+            return q_rows
+
+        def group_rows(c, b, q_rows, psum):
+            q_words = q_rows[:].bitcast(F32)
+            mt = psum.tile([P, 2, 2, P], F32, name="mt")
+            for e in range(2):
+                for u in range(2):
+                    nc.tensor.transpose(mt[:, e, u, :], q_words[:, e, u : CHANNELS // 2 : 2], ident[:])
+            gq = operands(c)[:, 0].rearrange("p (b w e t) -> p b w e t", b=CHUNK_IMAGES, e=2, t=PACK)
+            nc.scalar.copy(
+                out=gq[:, b].bitcast(F32),
+                in_=mt[:].rearrange("p e u w -> p w e u"),
+            )
+
+        def normalise(c, image, images, psum):
+            spread = psum.tile([P, images * PAIRS, 2], F32, name="spread")
+            for b in range(images):
+                for e in range(2):
+                    nc.tensor.transpose(
+                        spread[:, b * PAIRS : (b + 1) * PAIRS, e],
+                        inv_norms[c][:, image + b, e : e + 1].to_broadcast([P, P]),
+                        ident[:],
+                    )
+            pixels = slice(image * PIXELS, (image + images) * PIXELS)
+            gq = operands(c)[:, 0].rearrange("p (n t) -> p n t", t=PACK)
+            x = x_tiles[c][:].rearrange("p t b n -> p t (b n)")
             factor = spread[:].rearrange("p (l i) e -> p l (i e)", i=LINE // 2).unsqueeze(2)
             nc.vector.tensor_tensor(
-                out=gq[:, b].rearrange("p (l i) t -> p l t i", i=LINE),
-                in0=x_tiles[c][:, b].rearrange("p t (l i) -> p l t i", i=LINE),
-                in1=factor.to_broadcast([P, PIXELS // LINE, PACK, LINE]),
+                out=gq[:, pixels].rearrange("p (l i) t -> p l t i", i=LINE),
+                in0=x[:, :, pixels].rearrange("p t (l i) -> p l t i", i=LINE),
+                in1=factor.to_broadcast([P, images * PIXELS // LINE, PACK, LINE]),
                 op=ALU.mult,
             )
 
@@ -182,8 +220,8 @@ def tile_memory_sup_pb_t_kernel(
                 in_=g[:].rearrange("p g n -> p (g n)"),
             )
 
-        def convolve(c, banks):
-            y = banks.tile([P, CHUNK_PIXELS], F32, name="y")
+        def convolve(c, banks, tag="y"):
+            y = banks.tile([P, CHUNK_PIXELS], F32, name=tag)
             for g in range(GROUPS):
                 nc.tensor.matmul_mx(
                     out=y[:],
@@ -196,66 +234,108 @@ def tile_memory_sup_pb_t_kernel(
                 )
             return y
 
+        def vector_statistics(c, y):
+            i = c if c < SCALAR_CHUNKS[0] else c - len(SCALAR_CHUNKS)
+            nc.vector.bn_stats(out=stats[:, i * STATS : (i + 1) * STATS], in_=y[:])
+            if c == 0:
+                nc.vector.tensor_scalar_mul(out=minus_shift[:], in0=stats[:, 1:2], scalar1=-1.0)
+
+        def scalar_statistics(c, y):
+            i = SCALAR_CHUNKS.index(c)
+            for func, total in ((ACT.Identity, shifted_sum), (ACT.Square, shifted_squares)):
+                values = scrap.tile([P, CHUNK_PIXELS], BF16, name="squares")
+                nc.scalar.activation(
+                    out=values[:], in_=y[:], func=func, bias=minus_shift[:, 0:1], accum_out=total[:, i : i + 1]
+                )
+
+        def scalar_records():
+            n = len(SCALAR_CHUNKS)
+            records = stats[:, vector_stats:].rearrange("o (c r) -> o c r", r=RECORD)
+            mean = keep.tile([P, n], F32)
+            nc.vector.tensor_scalar_mul(out=mean[:], in0=shifted_sum[:], scalar1=1.0 / CHUNK_PIXELS)
+            nc.vector.memset(records[:, :, 0], float(CHUNK_PIXELS))
+            nc.vector.tensor_scalar(
+                out=records[:, :, 1], in0=mean[:], scalar1=minus_shift[:, 0:1], scalar2=None, op0=ALU.subtract
+            )
+            squared_mean = keep.tile([P, n], F32)
+            nc.vector.scalar_tensor_tensor(
+                out=squared_mean[:], in0=mean[:], scalar=-1.0, in1=shifted_sum[:], op0=ALU.mult, op1=ALU.mult
+            )
+            nc.vector.tensor_tensor(
+                out=records[:, :, 2], in0=squared_mean[:], in1=shifted_squares[:], op=ALU.add
+            )
+
         with tc.psum_pool(name="psum", bufs=2) as psum:
             for b in range(CHUNK_IMAGES):
                 square_sums(0, b, psum)
                 invert(0, b, 1)
             group_memory(0, psum, nc.vector.tensor_copy)
             square_sums(1, 0, psum)
-            normalise(0, 0, psum)
+            normalise(0, 0, 1, psum)
             square_sums(1, 1, psum)
             invert(1, 0, CHUNK_IMAGES)
-            normalise(0, 1, psum)
+            normalise(0, 1, 1, psum)
             group_memory(1, psum, nc.vector.tensor_copy)
             quantise(0)
             load(AHEAD)
             for step in range(2, CHUNKS + 3):
                 c = step - 2
-                if 1 <= c < CHUNKS:
+                if 1 <= c < CHUNKS - 1:
                     if c + AHEAD < CHUNKS:
                         load(c + AHEAD)
-                    for b in range(CHUNK_IMAGES):
-                        normalise(c, b, psum)
+                    normalise(c, 0, CHUNK_IMAGES, psum)
                 if step < CHUNKS:
-                    for b in range(CHUNK_IMAGES):
-                        square_sums(step, b, psum)
+                    last_pixels = [square_sums(step, b, psum) for b in range(CHUNK_IMAGES)]
                     invert(step, 0, CHUNK_IMAGES)
                 if c >= 1:
                     y = convolve(c - 1, psum)
-                    nc.vector.bn_stats(out=stats[:, c - 1, :], in_=y[:])
+                    if c == CHUNKS:
+                        scalar_records()
+                    if c - 1 not in SCALAR_CHUNKS:
+                        vector_statistics(c - 1, y)
                 if step < CHUNKS:
                     group_memory(step, psum, nc.scalar.copy)
+                if step == CHUNKS:
+                    for b in range(CHUNK_IMAGES):
+                        group_rows(step - 1, b, last_rows[b], psum)
+                if c - 1 in SCALAR_CHUNKS:
+                    scalar_statistics(c - 1, y)
+                if step == CHUNKS - 1:
+                    last_rows = [normalise_rows(step, b, last_pixels[b]) for b in range(CHUNK_IMAGES)]
                 if 1 <= c < CHUNKS:
                     quantise(c)
 
-        mean_var = keep.tile([P, 2], F32)
-        nc.vector.bn_aggr(out=mean_var[:], in_=stats[:].rearrange("o c s -> o (c s)"))
-        var_eps = keep.tile([P, 1], F32)
-        nc.vector.tensor_scalar_add(out=var_eps[:], in0=mean_var[:, 1:2], scalar1=BN_EPS)
-        std = keep.tile([P, 1], F32)
-        nc.scalar.activation(out=std[:], in_=var_eps[:], func=ACT.Sqrt)
-        rstd = keep.tile([P, 1], F32)
-        nc.vector.reciprocal(out=rstd[:], in_=std[:])
-        neg_mean = keep.tile([P, 1], F32)
-        nc.vector.tensor_scalar_mul(out=neg_mean[:], in0=mean_var[:, 0:1], scalar1=-1.0)
-        scale = keep.tile([P, 1], F32)
-        nc.vector.tensor_tensor(out=scale[:], in0=gamma[:], in1=rstd[:], op=ALU.mult)
-        shift = keep.tile([P, 1], F32)
-        nc.vector.scalar_tensor_tensor(
-            out=shift[:], in0=neg_mean[:], scalar=scale[:, 0:1], in1=beta[:], op0=ALU.mult, op1=ALU.add
-        )
-        with tc.psum_pool(name="again", bufs=PSUM_BANKS, reuse_waits="tile") as again:
+            mean_var = keep.tile([P, 2], F32)
+            nc.vector.bn_aggr(out=mean_var[:], in_=stats[:])
+            std = keep.tile([P, 1], F32)
+            nc.scalar.activation(out=std[:], in_=mean_var[:, 1:2], func=ACT.Sqrt, bias=eps[:, 0:1])
+            minus_mean_gamma = keep.tile([P, 1], F32)
+            nc.vector.scalar_tensor_tensor(
+                out=minus_mean_gamma[:], in0=mean_var[:, 0:1], scalar=-1.0, in1=gamma[:], op0=ALU.mult, op1=ALU.mult
+            )
+            rstd = keep.tile([P, 1], F32)
+            nc.vector.reciprocal(out=rstd[:], in_=std[:])
+            scale = keep.tile([P, 1], F32)
+            nc.vector.tensor_tensor(out=scale[:], in0=gamma[:], in1=rstd[:], op=ALU.mult)
+            shift = keep.tile([P, 1], F32)
+            nc.vector.scalar_tensor_tensor(
+                out=shift[:], in0=minus_mean_gamma[:], scalar=rstd[:, 0:1], in1=beta[:], op0=ALU.mult, op1=ALU.add
+            )
+
+            def finish_on_scalar(r, y):
+                nc.scalar.activation(out=r, in_=y, func=ACT.Relu, bias=shift[:, 0:1], scale=scale[:, 0:1])
+
+            def finish_on_vector(r, y):
+                nc.vector.tensor_scalar(
+                    out=r, in0=y, scalar1=scale[:, 0:1], scalar2=shift[:, 0:1], op0=ALU.mult, op1=ALU.add
+                )
+                nc.vector.tensor_scalar_max(out=r, in0=r, scalar1=0.0)
+
             for c in range(CHUNKS):
-                y = convolve(c, again)
-                r = result[:, c, :]
-                if c % 2 == 0:
-                    nc.scalar.activation(out=r, in_=y[:], func=ACT.Relu, bias=shift[:, 0:1], scale=scale[:, 0:1])
-                else:
-                    nc.vector.tensor_scalar(
-                        out=r, in0=y[:], scalar1=scale[:, 0:1], scalar2=shift[:, 0:1], op0=ALU.mult, op1=ALU.add
-                    )
-                    nc.vector.tensor_scalar_max(out=r, in0=r, scalar1=0.0)
+                y = convolve(c, psum, BANK_TAGS[c // 2 % len(BANK_TAGS)])
+                finish = finish_on_vector if c % 2 else finish_on_scalar
+                finish(result[:, c, :], y[:])
                 nc.sync.dma_start(
                     out=out[c * CHUNK_IMAGES : (c + 1) * CHUNK_IMAGES].rearrange("b o h w -> o b (h w)"),
-                    in_=r.rearrange("o (b n) -> o b n", b=CHUNK_IMAGES),
+                    in_=result[:, c, :].rearrange("o (b n) -> o b n", b=CHUNK_IMAGES),
                 )

@@ -30,7 +30,7 @@ STATS = 2 * RECORD
 SCALAR_CHUNKS = range(CHUNKS - 4, CHUNKS - 1)
 AHEAD = 7
 BANK_TAGS = ("xt", "mt", "spread", "y")
-LINE = 8
+RUN = 4
 
 FLOPS = 2 * BATCH * PIXELS * GROUPS * CHANNELS * OUT_CHANNELS
 
@@ -76,8 +76,9 @@ def tile_memory_sup_pb_t_kernel(
 
         def load_pixels(c, image, images):
             if c not in x_tiles:
-                x = loads.tile([P, PACK, CHUNK_IMAGES, PIXELS], BF16, name="x")
-                x_tiles[c] = x
+                x = loads.tile([P, PACK * CHUNK_IMAGES * PIXELS], BF16, name="x")
+                order = "(b t n)" if c == 0 else "(t b n)"
+                x_tiles[c] = x[:].rearrange("p " + order + " -> p t b n", t=PACK, b=CHUNK_IMAGES)
             for b in range(image, image + images):
                 nc.sync.dma_start(
                     out=x_tiles[c][:, :, b],
@@ -127,7 +128,7 @@ def tile_memory_sup_pb_t_kernel(
             if c not in sums:
                 sumsq = work.tile([P, CHUNK_IMAGES, 2], F32, name="sumsq")
                 sums[c] = sumsq
-            x_words = x_tiles[c][:].bitcast(F32)
+            x_words = x_tiles[c].bitcast(F32)
             xt = psum.tile([P, PACK, P], F32, name="xt")
             for t in range(PACK):
                 nc.tensor.transpose(xt[:, t, :], x_words[:, t, b, :], ident[:])
@@ -203,12 +204,12 @@ def tile_memory_sup_pb_t_kernel(
                     )
             pixels = slice(image * PIXELS, (image + images) * PIXELS)
             gq = operands(c)[:, 0].rearrange("p (n t) -> p n t", t=PACK)
-            x = x_tiles[c][:].rearrange("p t b n -> p t (b n)")
-            factor = spread[:].rearrange("p (l i) e -> p l (i e)", i=LINE // 2).unsqueeze(2)
+            x = x_tiles[c][:, :, image : image + images].rearrange("p t b n -> p t (b n)")
+            factor = spread[:].rearrange("p (l i) e -> p l (i e)", i=RUN // 2).unsqueeze(2)
             nc.vector.tensor_tensor(
-                out=gq[:, pixels].rearrange("p (l i) t -> p l t i", i=LINE),
-                in0=x[:, :, pixels].rearrange("p t (l i) -> p l t i", i=LINE),
-                in1=factor.to_broadcast([P, images * PIXELS // LINE, PACK, LINE]),
+                out=gq[:, pixels].rearrange("p (l i) t -> p l t i", i=RUN),
+                in0=x.rearrange("p t (l i) -> p l t i", i=RUN),
+                in1=factor.to_broadcast([P, images * PIXELS // RUN, PACK, RUN]),
                 op=ALU.mult,
             )
 

@@ -30,7 +30,7 @@ STATS = 2 * RECORD
 SCALAR_CHUNKS = range(CHUNKS - 4, CHUNKS - 1)
 AHEAD = 7
 BANK_TAGS = ("xt", "mt", "spread", "y")
-RUN = 4
+LINE = 8
 
 FLOPS = 2 * BATCH * PIXELS * GROUPS * CHANNELS * OUT_CHANNELS
 
@@ -76,14 +76,13 @@ def tile_memory_sup_pb_t_kernel(
 
         def load_pixels(c, image, images):
             if c not in x_tiles:
-                x = loads.tile([P, PACK * CHUNK_IMAGES * PIXELS], BF16, name="x")
-                order = "(b t n)" if c == 0 else "(t b n)"
-                x_tiles[c] = x[:].rearrange("p " + order + " -> p t b n", t=PACK, b=CHUNK_IMAGES)
-            for b in range(image, image + images):
-                nc.sync.dma_start(
-                    out=x_tiles[c][:, :, b],
-                    in_=query[c * CHUNK_IMAGES + b].rearrange("(p t) h w -> p t (h w)", t=PACK),
-                )
+                x = loads.tile([P, CHUNK_IMAGES, PACK, PIXELS], BF16, name="x")
+                x_tiles[c] = x
+            first = c * CHUNK_IMAGES + image
+            nc.sync.dma_start(
+                out=x_tiles[c][:, image : image + images].rearrange("p b t n -> p b (t n)"),
+                in_=query[first : first + images].rearrange("b (p t) h w -> p b (t h w)", t=PACK),
+            )
 
         def load_memory(c):
             m = loads.tile([P, ROW_BLOCKS, CHANNELS], BF16, name="m")
@@ -128,10 +127,10 @@ def tile_memory_sup_pb_t_kernel(
             if c not in sums:
                 sumsq = work.tile([P, CHUNK_IMAGES, 2], F32, name="sumsq")
                 sums[c] = sumsq
-            x_words = x_tiles[c].bitcast(F32)
+            x_words = x_tiles[c][:].bitcast(F32)
             xt = psum.tile([P, PACK, P], F32, name="xt")
             for t in range(PACK):
-                nc.tensor.transpose(xt[:, t, :], x_words[:, t, b, :], ident[:])
+                nc.tensor.transpose(xt[:, t, :], x_words[:, b, t, :], ident[:])
             by_pixel = xt[:].bitcast(BF16).rearrange("w t (p e) -> w t p e", e=2)
             for e in range(2):
                 squares = scrap.tile([P, PACK, P], BF16, name="squares")
@@ -193,23 +192,18 @@ def tile_memory_sup_pb_t_kernel(
                 in_=mt[:].rearrange("p e u w -> p w e u"),
             )
 
-        def normalise(c, image, images, psum):
-            spread = psum.tile([P, images * PAIRS, 2], F32, name="spread")
-            for b in range(images):
-                for e in range(2):
-                    nc.tensor.transpose(
-                        spread[:, b * PAIRS : (b + 1) * PAIRS, e],
-                        inv_norms[c][:, image + b, e : e + 1].to_broadcast([P, P]),
-                        ident[:],
-                    )
-            pixels = slice(image * PIXELS, (image + images) * PIXELS)
-            gq = operands(c)[:, 0].rearrange("p (n t) -> p n t", t=PACK)
-            x = x_tiles[c][:, :, image : image + images].rearrange("p t b n -> p t (b n)")
-            factor = spread[:].rearrange("p (l i) e -> p l (i e)", i=RUN // 2).unsqueeze(2)
+        def normalise(c, b, psum):
+            spread = psum.tile([P, PAIRS, 2], F32, name="spread")
+            for e in range(2):
+                nc.tensor.transpose(
+                    spread[:, :, e], inv_norms[c][:, b, e : e + 1].to_broadcast([P, P]), ident[:]
+                )
+            gq = operands(c)[:, 0].rearrange("p (b n t) -> p b n t", b=CHUNK_IMAGES, t=PACK)
+            factor = spread[:].rearrange("p (l i) e -> p l (i e)", i=LINE // 2).unsqueeze(2)
             nc.vector.tensor_tensor(
-                out=gq[:, pixels].rearrange("p (l i) t -> p l t i", i=RUN),
-                in0=x.rearrange("p t (l i) -> p l t i", i=RUN),
-                in1=factor.to_broadcast([P, images * PIXELS // RUN, PACK, RUN]),
+                out=gq[:, b].rearrange("p (l i) t -> p l t i", i=LINE),
+                in0=x_tiles[c][:, b].rearrange("p t (l i) -> p l t i", i=LINE),
+                in1=factor.to_broadcast([P, PIXELS // LINE, PACK, LINE]),
                 op=ALU.mult,
             )
 
@@ -272,10 +266,10 @@ def tile_memory_sup_pb_t_kernel(
                 invert(0, b, 1)
             group_memory(0, psum, nc.vector.tensor_copy)
             square_sums(1, 0, psum)
-            normalise(0, 0, 1, psum)
+            normalise(0, 0, psum)
             square_sums(1, 1, psum)
             invert(1, 0, CHUNK_IMAGES)
-            normalise(0, 1, 1, psum)
+            normalise(0, 1, psum)
             group_memory(1, psum, nc.vector.tensor_copy)
             quantise(0)
             load(AHEAD)
@@ -284,7 +278,8 @@ def tile_memory_sup_pb_t_kernel(
                 if 1 <= c < CHUNKS - 1:
                     if c + AHEAD < CHUNKS:
                         load(c + AHEAD)
-                    normalise(c, 0, CHUNK_IMAGES, psum)
+                    for b in range(CHUNK_IMAGES):
+                        normalise(c, b, psum)
                 if step < CHUNKS:
                     last_pixels = [square_sums(step, b, psum) for b in range(CHUNK_IMAGES)]
                     invert(step, 0, CHUNK_IMAGES)
@@ -334,9 +329,9 @@ def tile_memory_sup_pb_t_kernel(
 
             for c in range(CHUNKS):
                 y = convolve(c, psum, BANK_TAGS[c // 2 % len(BANK_TAGS)])
-                finish = finish_on_vector if c % 2 else finish_on_scalar
+                finish, queue = (finish_on_vector, nc.sync) if c % 2 else (finish_on_scalar, nc.scalar)
                 finish(result[:, c, :], y[:])
-                nc.sync.dma_start(
+                queue.dma_start(
                     out=out[c * CHUNK_IMAGES : (c + 1) * CHUNK_IMAGES].rearrange("b o h w -> o b (h w)"),
                     in_=result[:, c, :].rearrange("o (b n) -> o b n", b=CHUNK_IMAGES),
                 )

@@ -87,7 +87,9 @@ def tile_memory_sup_pb_t_kernel(
         def load_memory(c):
             m = loads.tile([P, ROW_BLOCKS, CHANNELS], BF16, name="m")
             rows = concat_memory[c * CHUNK_PIXELS : (c + 1) * CHUNK_PIXELS, :]
-            nc.sync.dma_start(out=m[:], in_=rows.rearrange("(j p) k -> p j k", p=P))
+            nc.sync.dma_start(
+                out=m[:].rearrange("p j k -> p (j k)"), in_=rows.rearrange("(p j) k -> p (j k)", j=ROW_BLOCKS)
+            )
             m_tiles[c] = m
 
         def load(c):
@@ -107,11 +109,11 @@ def tile_memory_sup_pb_t_kernel(
                 out=w_scales[32 * quad : 32 * quad + 4].bitcast(I32),
                 in_=conv_w_scales.bitcast(I32)[:, 4 * quad : 4 * quad + 4, :].rearrange("g r n -> r g n"),
             )
-        with nc.allow_non_contiguous_dma(reason="128 gains and shifts, one to a partition"):
-            nc.scalar.dma_start(out=gamma[:], in_=bn_gamma.rearrange("(o one) -> o one", one=1))
-            nc.scalar.dma_start(out=beta[:], in_=bn_beta.rearrange("(o one) -> o one", one=1))
         for c in range(2, AHEAD):
             load(c)
+        with nc.allow_non_contiguous_dma(reason="128 gains and shifts, one to a partition"):
+            nc.sync.dma_start(out=gamma[:], in_=bn_gamma.rearrange("(o one) -> o one", one=1))
+            nc.sync.dma_start(out=beta[:], in_=bn_beta.rearrange("(o one) -> o one", one=1))
 
         sums = {}
         inv_norms = {}
@@ -155,7 +157,7 @@ def tile_memory_sup_pb_t_kernel(
 
         def group_memory(c, psum, copy):
             m_words = m_tiles[c][:].bitcast(F32)
-            rows = operands(c)[:, 1].rearrange("p (j r t) -> p j r t", j=ROW_BLOCKS, t=PACK)
+            rows = operands(c)[:, 1].rearrange("p (r j t) -> p r j t", j=ROW_BLOCKS, t=PACK)
             gm_words = rows.bitcast(F32)
             for half in range(ROW_BLOCKS // 2):
                 mt = psum.tile([P, 2, 2, P], F32, name="mt")
@@ -165,8 +167,8 @@ def tile_memory_sup_pb_t_kernel(
                             mt[:, jj, u, :], m_words[:, 2 * half + jj, u : CHANNELS // 2 : 2], ident[:]
                         )
                 copy(
-                    out=gm_words[:, 2 * half : 2 * half + 2],
-                    in_=mt[:].rearrange("p j u r -> p j r u"),
+                    out=gm_words[:, :, 2 * half : 2 * half + 2],
+                    in_=mt[:].rearrange("p j u r -> p r j u"),
                 )
 
         def normalise_rows(c, b, by_pixel):

from contextlib import ExitStack

import concourse.mybir as mybir
from concourse.masks import make_identity

F32 = mybir.dt.float32
BF16 = mybir.dt.bfloat16
I32 = mybir.dt.int32
U32 = mybir.dt.uint32
U8 = mybir.dt.uint8
FP8X4 = mybir.dt.float8_e4m3fn_x4
FP4X4 = mybir.dt.float4_e2m1fn_x4
ACT = mybir.ActivationFunctionType
ALU = mybir.AluOpType

P = 128
PACK = 4
BATCH, CHANNELS, PIXELS = 32, 512, 256
OUT_CHANNELS = 128
GROUPS = 2
PAIRS = PIXELS // 2
CHUNK_IMAGES = 2
CHUNK_PIXELS = CHUNK_IMAGES * PIXELS
CHUNKS = BATCH // CHUNK_IMAGES
ROW_BLOCKS = CHUNK_PIXELS // P
L2_EPS = 1e-12
BN_EPS = 1e-5
RECORD = 3
STATS = 2 * RECORD
SCALAR_CHUNKS = range(CHUNKS - 4, CHUNKS - 1)
AHEAD = 7
BANK_TAGS = ("xt", "mt", "spread", "y")
LINE = 8

FLOPS = 2 * BATCH * PIXELS * GROUPS * CHANNELS * OUT_CHANNELS


def tile_memory_sup_pb_t_kernel(
    tc, query, concat_memory, conv_w_words, conv_w_scales, bn_gamma, bn_beta, out
):
    nc = tc.nc
    with ExitStack() as stack:
        keep = stack.enter_context(tc.tile_pool(name="keep", bufs=1))
        loads = stack.enter_context(tc.tile_pool(name="loads", bufs=AHEAD))
        work = stack.enter_context(tc.tile_pool(name="work", bufs=3))
        scrap = stack.enter_context(tc.tile_pool(name="scrap", bufs=4))
        stack.enter_context(tc.manual_schedule())

        ident = keep.tile([P, P], F32)
        make_identity(nc, ident[:])
        w_words = keep.tile([P, GROUPS, 2 * OUT_CHANNELS], U8, align_bytes=64)
        w_scales = keep.tile([P, GROUPS, OUT_CHANNELS], U8, align_bytes=64)
        nc.vector.memset(w_scales[:].bitcast(I32), 0)
        gamma = keep.tile([P, 1], BF16)
        beta = keep.tile([P, 1], BF16)
        result = keep.tile([P, CHUNKS, CHUNK_PIXELS], F32)
        codes = keep.tile([P, CHUNKS, GROUPS, CHUNK_PIXELS], U32, align_bytes=64)
        scales = keep.tile([P, CHUNKS, GROUPS, CHUNK_PIXELS], U8, align_bytes=64)
        vector_stats = (CHUNKS - len(SCALAR_CHUNKS)) * STATS
        stats = keep.tile([P, vector_stats + len(SCALAR_CHUNKS) * RECORD], F32)
        minus_shift = keep.tile([P, 1], F32)
        shifted_sum = keep.tile([P, len(SCALAR_CHUNKS)], F32)
        shifted_squares = keep.tile([P, len(SCALAR_CHUNKS)], F32)
        minus_half = keep.tile([P, CHUNK_IMAGES, 2], F32)
        nc.gpsimd.memset(minus_half[:], -0.5)
        eps = keep.tile([P, 1], F32)
        nc.vector.memset(eps[:], 0.0)
        nc.vector.tensor_scalar_add(out=eps[:], in0=eps[:], scalar1=BN_EPS)
        one = keep.tile([P, 1], F32)
        nc.vector.memset(one[:], 1.0)
        root_of_one = keep.tile([P, 1], F32)
        nc.scalar.activation(out=root_of_one[:], in_=one[:], func=ACT.Sqrt)

        x_tiles = {}
        m_tiles = {}

        def load_pixels(c, image, images):
            if c not in x_tiles:
                x = loads.tile([P, CHUNK_IMAGES, PACK, PIXELS], BF16, name="x")
                x_tiles[c] = x
            first = c * CHUNK_IMAGES + image
            nc.sync.dma_start(
                out=x_tiles[c][:, image : image + images].rearrange("p b t n -> p b (t n)"),
                in_=query[first : first + images].rearrange("b (p t) h w -> p b (t h w)", t=PACK),
            )

        def load_memory(c):
            m = loads.tile([P, ROW_BLOCKS, CHANNELS], BF16, name="m")
            rows = concat_memory[c * CHUNK_PIXELS : (c + 1) * CHUNK_PIXELS, :]
            nc.sync.dma_start(
                out=m[:].rearrange("p j k -> p (j k)"), in_=rows.rearrange("(p j) k -> p (j k)", j=ROW_BLOCKS)
            )
            m_tiles[c] = m

        def load(c):
            load_pixels(c, 0, CHUNK_IMAGES)
            load_memory(c)

        for b in range(CHUNK_IMAGES):
            load_pixels(0, b, 1)
        load_memory(0)
        load(1)
        nc.sync.dma_start(
            out=w_words[:].bitcast(I32),
            in_=conv_w_words.bitcast(I32).rearrange("g p n -> p g n"),
        )
        for quad in range(4):
            nc.sync.dma_start(
                out=w_scales[32 * quad : 32 * quad + 4].bitcast(I32),
                in_=conv_w_scales.bitcast(I32)[:, 4 * quad : 4 * quad + 4, :].rearrange("g r n -> r g n"),
            )
        for c in range(2, AHEAD):
            load(c)
        with nc.allow_non_contiguous_dma(reason="128 gains and shifts, one to a partition"):
            nc.sync.dma_start(out=gamma[:], in_=bn_gamma.rearrange("(o one) -> o one", one=1))
            nc.sync.dma_start(out=beta[:], in_=bn_beta.rearrange("(o one) -> o one", one=1))

        sums = {}
        inv_norms = {}
        grouped = {}

        def operands(c):
            if c not in grouped:
                g = work.tile([P, GROUPS, CHUNK_PIXELS * PACK], BF16, name="g", align_bytes=64)
                grouped[c] = g
            return grouped[c]

        def square_sums(c, b, psum):
            if c not in sums:
                sumsq = work.tile([P, CHUNK_IMAGES, 2], F32, name="sumsq")
                sums[c] = sumsq
            x_words = x_tiles[c][:].bitcast(F32)
            xt = psum.tile([P, PACK, P], F32, name="xt")
            for t in range(PACK):
                nc.tensor.transpose(xt[:, t, :], x_words[:, b, t, :], ident[:])
            by_pixel = xt[:].bitcast(BF16).rearrange("w t (p e) -> w t p e", e=2)
            for e in range(2):
                squares = scrap.tile([P, PACK, P], BF16, name="squares")
                nc.scalar.activation(
                    out=squares[:],
                    in_=by_pixel[:, :, :, e],
                    func=ACT.Square,
                    accum_out=sums[c][:, b, e : e + 1],
                )
            return by_pixel

        def invert(c, image, images):
            if c not in inv_norms:
                inv_norm = work.tile([P, CHUNK_IMAGES, 2], F32, name="inv_norm")
                inv_norms[c] = inv_norm
            part = slice(image, image + images)
            floored = work.tile([P, images, 2], F32, name="floored")
            nc.gpsimd.tensor_scalar_max(out=floored[:], in0=sums[c][:, part], scalar1=L2_EPS * L2_EPS)
            nc.gpsimd.tensor_tensor(
                out=inv_norms[c][:, part], in0=floored[:], in1=minus_half[:, part], op=ALU.pow
            )

        def group_memory(c, psum, copy):
            m_words = m_tiles[c][:].bitcast(F32)
            rows = operands(c)[:, 1].rearrange("p (r j t) -> p r j t", j=ROW_BLOCKS, t=PACK)
            gm_words = rows.bitcast(F32)
            for half in range(ROW_BLOCKS // 2):
                mt = psum.tile([P, 2, 2, P], F32, name="mt")
                for jj in range(2):
                    for u in range(2):
                        nc.tensor.transpose(
                            mt[:, jj, u, :], m_words[:, 2 * half + jj, u : CHANNELS // 2 : 2], ident[:]
                        )
                copy(
                    out=gm_words[:, :, 2 * half : 2 * half + 2],
                    in_=mt[:].rearrange("p j u r -> p r j u"),
                )

        def normalise_rows(c, b, by_pixel):
            q_rows = work.tile([P, 2, CHANNELS], BF16, name="q_rows")
            for e in range(2):
                nc.scalar.activation(
                    out=q_rows[:, e].rearrange("w (p t) -> w p t", t=PACK),
                    in_=by_pixel[:, :, :, e].rearrange("w t p -> w p t"),
                    func=ACT.Copy,
                    scale=inv_norms[c][:, b, e : e + 1],
                )
            return q_rows

        def group_rows(c, b, q_rows, psum):
            q_words = q_rows[:].bitcast(F32)
            mt = psum.tile([P, 2, 2, P], F32, name="mt")
            for e in range(2):
                for u in range(2):
                    nc.tensor.transpose(mt[:, e, u, :], q_words[:, e, u : CHANNELS // 2 : 2], ident[:])
            gq = operands(c)[:, 0].rearrange("p (b w e t) -> p b w e t", b=CHUNK_IMAGES, e=2, t=PACK)
            nc.scalar.copy(
                out=gq[:, b].bitcast(F32),
                in_=mt[:].rearrange("p e u w -> p w e u"),
            )

        def normalise(c, b, psum):
            spread = psum.tile([P, PAIRS, 2], F32, name="spread")
            for e in range(2):
                nc.tensor.transpose(
                    spread[:, :, e], inv_norms[c][:, b, e : e + 1].to_broadcast([P, P]), ident[:]
                )
            gq = operands(c)[:, 0].rearrange("p (b n t) -> p b n t", b=CHUNK_IMAGES, t=PACK)
            factor = spread[:].rearrange("p (l i) e -> p l (i e)", i=LINE // 2).unsqueeze(2)
            nc.vector.tensor_tensor(
                out=gq[:, b].rearrange("p (l i) t -> p l t i", i=LINE),
                in0=x_tiles[c][:, b].rearrange("p t (l i) -> p l t i", i=LINE),
                in1=factor.to_broadcast([P, PIXELS // LINE, PACK, LINE]),
                op=ALU.mult,
            )

        def quantise(c):
            g = grouped.pop(c)
            nc.vector.quantize_mx(
                out=codes[:, c].rearrange("p g n -> p (g n)").bitcast(FP8X4),
                scales=scales[:, c].rearrange("p g n -> p (g n)"),
                in_=g[:].rearrange("p g n -> p (g n)"),
            )

        def convolve(c, banks, tag="y"):
            y = banks.tile([P, CHUNK_PIXELS], F32, name=tag)
            for g in range(GROUPS):
                nc.tensor.matmul_mx(
                    out=y[:],
                    lhsT=w_words[:, g, :].bitcast(FP4X4),
                    lhsT_scale=w_scales[:, g, :],
                    rhs=codes[:, c, g, :].bitcast(FP8X4),
                    rhs_scale=scales[:, c, g, :],
                    start=(g == 0),
                    stop=(g == GROUPS - 1),
                )
            return y

        def vector_statistics(c, y):
            i = c if c < SCALAR_CHUNKS[0] else c - len(SCALAR_CHUNKS)
            nc.vector.bn_stats(out=stats[:, i * STATS : (i + 1) * STATS], in_=y[:])
            if c == 0:
                nc.vector.tensor_scalar_mul(out=minus_shift[:], in0=stats[:, 1:2], scalar1=-1.0)

        def scalar_statistics(c, y):
            i = SCALAR_CHUNKS.index(c)
            for func, total in ((ACT.Identity, shifted_sum), (ACT.Square, shifted_squares)):
                values = scrap.tile([P, CHUNK_PIXELS], BF16, name="squares")
                nc.scalar.activation(
                    out=values[:], in_=y[:], func=func, bias=minus_shift[:, 0:1], accum_out=total[:, i : i + 1]
                )

        def scalar_records():
            n = len(SCALAR_CHUNKS)
            records = stats[:, vector_stats:].rearrange("o (c r) -> o c r", r=RECORD)
            mean = keep.tile([P, n], F32)
            nc.vector.tensor_scalar_mul(out=mean[:], in0=shifted_sum[:], scalar1=1.0 / CHUNK_PIXELS)
            nc.vector.memset(records[:, :, 0], float(CHUNK_PIXELS))
            nc.vector.tensor_scalar(
                out=records[:, :, 1], in0=mean[:], scalar1=minus_shift[:, 0:1], scalar2=None, op0=ALU.subtract
            )
            squared_mean = keep.tile([P, n], F32)
            nc.vector.scalar_tensor_tensor(
                out=squared_mean[:], in0=mean[:], scalar=-1.0, in1=shifted_sum[:], op0=ALU.mult, op1=ALU.mult
            )
            nc.vector.tensor_tensor(
                out=records[:, :, 2], in0=squared_mean[:], in1=shifted_squares[:], op=ALU.add
            )

        with tc.psum_pool(name="psum", bufs=2) as psum:
            for b in range(CHUNK_IMAGES):
                square_sums(0, b, psum)
                invert(0, b, 1)
            group_memory(0, psum, nc.vector.tensor_copy)
            square_sums(1, 0, psum)
            normalise(0, 0, psum)
            square_sums(1, 1, psum)
            invert(1, 0, CHUNK_IMAGES)
            normalise(0, 1, psum)
            group_memory(1, psum, nc.vector.tensor_copy)
            quantise(0)
            load(AHEAD)
            for step in range(2, CHUNKS + 3):
                c = step - 2
                if 1 <= c < CHUNKS - 1:
                    if c + AHEAD < CHUNKS:
                        load(c + AHEAD)
                    for b in range(CHUNK_IMAGES):
                        normalise(c, b, psum)
                if step < CHUNKS:
                    last_pixels = [square_sums(step, b, psum) for b in range(CHUNK_IMAGES)]
                    invert(step, 0, CHUNK_IMAGES)
                if c >= 1:
                    y = convolve(c - 1, psum)
                    if c == CHUNKS:
                        scalar_records()
                    if c - 1 not in SCALAR_CHUNKS:
                        vector_statistics(c - 1, y)
                if step < CHUNKS:
                    group_memory(step, psum, nc.scalar.copy)
                if step == CHUNKS:
                    for b in range(CHUNK_IMAGES):
                        group_rows(step - 1, b, last_rows[b], psum)
                if c - 1 in SCALAR_CHUNKS:
                    scalar_statistics(c - 1, y)
                if step == CHUNKS - 1:
                    last_rows = [normalise_rows(step, b, last_pixels[b]) for b in range(CHUNK_IMAGES)]
                if 1 <= c < CHUNKS:
                    quantise(c)

            mean_var = keep.tile([P, 2], F32)
            nc.vector.bn_aggr(out=mean_var[:], in_=stats[:])
            std = keep.tile([P, 1], F32)
            nc.scalar.activation(out=std[:], in_=mean_var[:, 1:2], func=ACT.Sqrt, bias=eps[:, 0:1])
            minus_mean_gamma = keep.tile([P, 1], F32)
            nc.vector.scalar_tensor_tensor(
                out=minus_mean_gamma[:], in0=mean_var[:, 0:1], scalar=-1.0, in1=gamma[:], op0=ALU.mult, op1=ALU.mult
            )
            rstd = keep.tile([P, 1], F32)
            nc.vector.reciprocal(out=rstd[:], in_=std[:])
            scale = keep.tile([P, 1], F32)
            nc.vector.tensor_tensor(out=scale[:], in0=gamma[:], in1=rstd[:], op=ALU.mult)
            shift = keep.tile([P, 1], F32)
            nc.vector.scalar_tensor_tensor(
                out=shift[:], in0=minus_mean_gamma[:], scalar=rstd[:, 0:1], in1=beta[:], op0=ALU.mult, op1=ALU.add
            )

            def finish_on_scalar(r, y):
                nc.scalar.activation(out=r, in_=y, func=ACT.Relu, bias=shift[:, 0:1], scale=scale[:, 0:1])

            def finish_on_vector(r, y):
                nc.vector.tensor_scalar(
                    out=r, in0=y, scalar1=scale[:, 0:1], scalar2=shift[:, 0:1], op0=ALU.mult, op1=ALU.add
                )
                nc.vector.tensor_scalar_max(out=r, in0=r, scalar1=0.0)

            for c in range(CHUNKS):
                y = convolve(c, psum, BANK_TAGS[c // 2 % len(BANK_TAGS)])
                finish, queue = (finish_on_vector, nc.sync) if c % 2 else (finish_on_scalar, nc.scalar)
                finish(result[:, c, :], y[:])
                queue.dma_start(
                    out=out[c * CHUNK_IMAGES : (c + 1) * CHUNK_IMAGES].rearrange("b o h w -> o b (h w)"),
                    in_=result[:, c, :].rearrange("o (b n) -> o b n", b=CHUNK_IMAGES),
                )
